import numpy as np
import ml_dtypes


def mxq(x, axis, fmt="e4m3"):
    dtype, down = {"e4m3": (ml_dtypes.float8_e4m3fn, 7), "e5m2": (ml_dtypes.float8_e5m2, 14)}[fmt]
    v = np.moveaxis(np.asarray(x, np.float32).astype(ml_dtypes.bfloat16).astype(np.float64), axis, -1)
    blocks = v.reshape(v.shape[:-1] + (-1, 32))
    amax = np.abs(blocks).max(-1, keepdims=True)
    byte = np.maximum(np.where(amax > 0, np.frexp(amax)[1] - 1 + 127, 0) - down, 1)
    scale = np.exp2(byte - 127.0)
    codes = (blocks / scale).astype(np.float32).astype(dtype).astype(np.float64)
    return np.moveaxis((codes * scale).reshape(v.shape), -1, axis)


WIDE = False


def mx_kscale(k):
    if not WIDE:
        return np.ones(k)
    levels = np.array([10, -10, 5, -5, 0])
    if k % 512:
        return np.exp2(np.random.permutation(np.resize(levels, k // 32))).repeat(32)
    a = np.empty((k // 512, 16))
    for p in range(k // 512):
        a[p, :8] = np.random.permutation(np.resize(levels, 8))
        for g in range(8):
            far = levels[np.abs(levels - a[p, g]) >= 10]
            a[p, g + 8] = far[np.random.randint(len(far))]
    return np.exp2(a.ravel()).repeat(32)


BF16 = ml_dtypes.bfloat16


def bf(x):
    return np.asarray(x, np.float32).astype(BF16)


def f64(x):
    return np.asarray(x).astype(np.float64)


B, N, R, DE, DR, NUM_BASES, OUT_DIM = 1, 1024, 16, 128, 64, 256, 128
F = DE + DR
KS = R * F


def draw0():
    s = mx_kscale(N)
    t = mx_kscale(KS)[:F]
    deg = np.random.uniform(0.5, 1.5, (B, R, N, 1))
    adj = np.random.uniform(0.0, 1.0, (B, R, N, N)) * deg / np.sqrt(N)
    return {"node_features": bf(np.random.standard_normal((B, N, DE)) * 2.0 / s[:, None] * t[:DE]),
            "relation_features": bf(np.random.standard_normal((B, R, DR)) * 2.0 / np.sqrt(N) / s.mean() * t[DE:]),
            "adj": bf(adj * s),
            "Wb": bf(np.random.standard_normal((NUM_BASES, KS)) / np.sqrt(KS) / np.tile(t, R))}


def core(node_features, relation_features, adj, Wb):
    a = f64(adj)
    node_part = mxq(a, 3, "e4m3") @ mxq(f64(node_features), 1, "e4m3")[:, None]
    row_sum = a.sum(-1)
    rel_part = row_sum[..., None] * f64(relation_features)[:, :, None, :]
    supports = np.concatenate([node_part, rel_part], -1)
    supports = supports.transpose(0, 2, 1, 3).reshape(B, N, KS)
    return mxq(supports, 2, "e4m3") @ mxq(f64(Wb), 1, "e4m3").T


def e4m3fn_bytes(y):
    return np.clip(np.asarray(y, np.float64), -448.0, 448.0).astype(np.float32).astype(ml_dtypes.float8_e4m3fn).view(np.uint8)


def e4m3fn_values(b):
    return np.asarray(b, np.uint8).view(ml_dtypes.float8_e4m3fn).astype(np.float64)


def setup_inputs():
    d = draw0()
    x0 = np.asarray(d['Wb']).astype(np.float64)
    s = (np.max(np.abs(x0), axis=(0,), keepdims=True) / 448.0).astype(np.float32)
    out = {}
    for k, v in d.items():
        if k == 'Wb':
            out['Wb_bytes'] = e4m3fn_bytes(x0 / s.astype(np.float64))
            out['Wb_scale'] = s
        else:
            out[k] = v
    return out


def reference(node_features, relation_features, adj, Wb_bytes, Wb_scale):
    return core(node_features, relation_features, adj, e4m3fn_values(Wb_bytes) * Wb_scale.astype(np.float64))

@@ -1,0 +1,372 @@
+from contextlib import ExitStack
+
+import concourse.mybir as mybir
+from concourse.masks import make_identity
+
+N = 1024
+R = 16
+DE = 128
+DR = 64
+F = DE + DR
+NB = 256
+P = 128
+IT = N // P
+RG = 4
+GROUPS = R // RG
+STEPS = IT * GROUPS
+PREFETCH = 5
+TENSOR_SUMS = (2, 1, 1, 0)
+
+F32 = mybir.dt.float32
+BF16 = mybir.dt.bfloat16
+U32 = mybir.dt.uint32
+U8 = mybir.dt.uint8
+FP8 = mybir.dt.float8_e4m3fn
+FP8X4 = mybir.dt.float8_e4m3fn_x4
+MULT = mybir.AluOpType.mult
+ADD = mybir.AluOpType.add
+
+FLOPS = 2 * (R * N * N * DE + N * R * F * NB)
+
+
+def tile_relationalgraphconvolution_pa_kernel(
+    tc, node_features, relation_features, adj, Wb_bytes, Wb_scale, out
+):
+    nc = tc.nc
+    with ExitStack() as ctx:
+        keep = ctx.enter_context(tc.tile_pool(name="keep", bufs=1))
+        rawp = ctx.enter_context(tc.tile_pool(name="rawp", bufs=PREFETCH + 1))
+        work = ctx.enter_context(tc.tile_pool(name="work", bufs=2))
+        late = ctx.enter_context(tc.tile_pool(name="late", bufs=6))
+        xtp = ctx.enter_context(tc.psum_pool(name="xtp", bufs=4))
+        mxp = ctx.enter_context(tc.psum_pool(name="mxp", bufs=2))
+        rsp = ctx.enter_context(tc.psum_pool(name="rsp", bufs=1))
+        outp = ctx.enter_context(tc.psum_pool(name="outp", bufs=1))
+        ctx.enter_context(tc.manual_schedule())
+
+        ident = keep.tile([P, P], F32, name="ident", align_bytes=64)
+        make_identity(nc, ident[:])
+
+        ones = keep.tile([P, 1], BF16, name="ones", align_bytes=64)
+        nc.gpsimd.memset(ones[:], 1.0)
+        nf_raw = keep.tile([P, 2, 4, DE], BF16, name="nf_raw", align_bytes=64)
+        nf_grp = keep.tile([P, 2, DE, 4], BF16, name="nf_grp", align_bytes=64)
+        nf_codes = keep.tile([P, 2 * DE], U32, name="nf_codes", align_bytes=64)
+        nf_scales = keep.tile([P, 2 * DE], U8, name="nf_scales", align_bytes=64)
+        relf = keep.tile([P, R * DR], BF16, name="relf", align_bytes=64)
+        w_bytes = keep.tile([P, 2 * R * F], U8, name="w_bytes", align_bytes=64)
+        w_scale = keep.tile([P, R * F], F32, name="w_scale", align_bytes=64)
+        w_val = keep.tile([P, 2 * R * F], BF16, name="w_val", align_bytes=64)
+        w_grp = keep.tile([P, 6 * NB * 4], BF16, name="w_grp", align_bytes=64)
+        w_codes = keep.tile([P, 6 * NB], U32, name="w_codes", align_bytes=64)
+        w_scales = keep.tile([P, 6 * NB], U8, name="w_scales", align_bytes=64)
+
+        raw = {}
+        perm = {}
+        grp = {}
+        codes = {}
+        scales = {}
+        mx = {}
+        rs = {}
+        supn = {}
+        supr = {}
+        sgrp = {}
+        scodes = {}
+        sscales = {}
+        obank = {}
+
+        def load(s, pieces=1):
+            it, g = s // GROUPS, s % GROUPS
+            raw[s] = rawp.tile([P, RG, N], BF16, name="raw", align_bytes=64)
+            n = RG // pieces
+            for a in range(pieces):
+                r0 = g * RG + a * n
+                nc.sync.dma_start(
+                    out=raw[s][:, a * n : (a + 1) * n, :],
+                    in_=adj[0, r0 : r0 + n, it * P : (it + 1) * P, :].rearrange("r i j -> i r j"),
+                )
+
+        def load_weight_bytes(h, f0, width):
+            c0 = h * R * F + f0 * R
+            rows = Wb_bytes[h * P : (h + 1) * P, :].rearrange("n (r f) -> n r f", f=F)
+            nc.sync.dma_start(
+                out=w_bytes[:, c0 : c0 + R * width].rearrange("p (r d) -> p r d", d=width),
+                in_=rows[:, :, f0 : f0 + width],
+            )
+
+        def load_weight_scale(f0, width):
+            sc = Wb_scale.rearrange("o (r f) -> (o r) f", f=F)
+            nc.sync.dma_start(
+                out=w_scale[:, f0 * R : f0 * R + R * width].rearrange("p (r d) -> p r d", d=width),
+                in_=sc[:, f0 : f0 + width].partition_broadcast(P),
+            )
+
+        def row_sums(s):
+            it, g = s // GROUPS, s % GROUPS
+            if g == 0:
+                rs[it] = late.tile([P, R], F32, name="rs")
+                supn[it] = work.tile([P, R * DE], BF16, name="supn", align_bytes=64)
+                supr[it] = work.tile([P, R * DR], BF16, name="supr", align_bytes=64)
+            perm[s] = work.tile([P, RG * N], BF16, name="perm", align_bytes=64)
+            for a in range(RG - TENSOR_SUMS[g]):
+                r = g * RG + a
+                nc.vector.tensor_scalar(
+                    out=perm[s][:, a * N : (a + 1) * N].rearrange("p (u q e) -> p u q e", u=2, e=2),
+                    in0=raw[s][:, a, :].rearrange("p (q u e) -> p u q e", u=2, e=2),
+                    scalar1=1.0,
+                    scalar2=None,
+                    op0=MULT,
+                    op1=ADD,
+                    accum_out=rs[it][:, r : r + 1],
+                )
+            relation_part(it, g * RG, RG - TENSOR_SUMS[g])
+
+        def relation_part(it, r0, n):
+            c0 = r0 * DR
+            nc.gpsimd.tensor_tensor(
+                out=supr[it][:, c0 : c0 + n * DR].rearrange("p (r d) -> p r d", d=DR),
+                in0=relf[:, c0 : c0 + n * DR].rearrange("p (r d) -> p r d", d=DR),
+                in1=rs[it][:, r0 : r0 + n].unsqueeze(2).to_broadcast([P, n, DR]),
+                op=MULT,
+            )
+
+        def tensor_sums(s):
+            it, g = s // GROUPS, s % GROUPS
+            n = TENSOR_SUMS[g]
+            if n == 0:
+                return
+            bank = rsp.tile([P, 512], F32, name="rsb")
+            for b in range(n):
+                a = RG - n + b
+                tile4 = grp[s][:, a * N : (a + 1) * N].rearrange("p (c i t) -> p c i t", c=2, t=4)
+                for c in range(2):
+                    for t in range(4):
+                        nc.tensor.matmul(
+                            bank[:, b : b + 1],
+                            lhsT=tile4[:, c, :, t],
+                            rhs=ones[:],
+                            start=(c == 0 and t == 0),
+                            stop=(c == 1 and t == 3),
+                        )
+            r0 = (g + 1) * RG - n
+            nc.scalar.copy(out=rs[it][:, r0 : r0 + n], in_=bank[:, 0:n])
+            relation_part(it, r0, n)
+
+        def turn(s):
+            grp[s] = work.tile([P, RG * N], BF16, name="grp", align_bytes=64)
+            for a in range(RG):
+                bank = xtp.tile([P, 512], F32, name="xt")
+                for c in range(2):
+                    for u in range(2):
+                        k0 = (c * 2 + u) * P
+                        if a < RG - TENSOR_SUMS[s % GROUPS]:
+                            w0 = a * 512 + u * 256 + c * P
+                            src = perm[s][:].bitcast(F32)[:, w0 : w0 + P]
+                        else:
+                            src = raw[s][:, a, :].bitcast(F32)[:, c * 256 + u : (c + 1) * 256 : 2]
+                        nc.tensor.transpose(bank[:, k0 : k0 + P], src, ident[:])
+                nc.scalar.copy(
+                    out=grp[s][:, a * N : (a + 1) * N].bitcast(F32).rearrange("p (c i u) -> p c i u", c=2, u=2),
+                    in_=bank[:].rearrange("p (c u i) -> p c i u", c=2, u=2),
+                )
+
+        def quantise(s, a0=0, n=RG):
+            if a0 == 0:
+                codes[s] = work.tile([P, N], U32, name="codes", align_bytes=64)
+                scales[s] = work.tile([P, N], U8, name="scales", align_bytes=64)
+            cols = slice(a0 * 256, (a0 + n) * 256)
+            nc.vector.quantize_mx(
+                out=codes[s][:, cols].bitcast(FP8X4),
+                scales=scales[s][:, cols],
+                in_=grp[s][:, a0 * N : (a0 + n) * N],
+            )
+
+        def aggregate(s, a0=0, n=RG):
+            if a0 == 0:
+                mx[s] = mxp.tile([P, RG * DE], F32, name="mx")
+            for a in range(a0, a0 + n):
+                for c in range(2):
+                    cols = slice(a * 256 + c * P, a * 256 + (c + 1) * P)
+                    nf_cols = slice(c * DE, (c + 1) * DE)
+                    nc.tensor.matmul_mx(
+                        out=mx[s][:, a * DE : (a + 1) * DE],
+                        lhsT=codes[s][:, cols].bitcast(FP8X4),
+                        lhsT_scale=scales[s][:, cols],
+                        rhs=nf_codes[:, nf_cols].bitcast(FP8X4),
+                        rhs_scale=nf_scales[:, nf_cols],
+                        start=(c == 0),
+                        stop=(c == 1),
+                    )
+
+        def keep_supports(s, a0=0, n=RG):
+            it, g = s // GROUPS, s % GROUPS
+            dst = supn[it][:, g * 512 : (g + 1) * 512].rearrange("p (u q e) -> p u q e", u=2, e=2)
+            nc.scalar.copy(
+                out=dst[:, :, a0 * 32 : (a0 + n) * 32, :],
+                in_=mx[s][:, a0 * DE : (a0 + n) * DE].rearrange("p (q u e) -> p u q e", u=2, e=2),
+            )
+
+        def turn_supports(it, q0, n):
+            if q0 == 0:
+                sgrp[it] = work.tile([P, 6 * 512], BF16, name="sgrp", align_bytes=64)
+            bank = xtp.tile([P, 512], F32, name="xt")
+            for b in range(n):
+                for u in range(2):
+                    k0 = (b * 2 + u) * P
+                    q = q0 + b
+                    if q < 4:
+                        w0 = q * 256 + u * P
+                        src = supn[it][:].bitcast(F32)[:, w0 : w0 + P]
+                    else:
+                        w0 = (q - 4) * 256
+                        src = supr[it][:].bitcast(F32)[:, w0 + u : w0 + 256 : 2]
+                    nc.tensor.transpose(bank[:, k0 : k0 + P], src, ident[:])
+            nc.scalar.copy(
+                out=sgrp[it][:, q0 * 512 : (q0 + n) * 512]
+                .bitcast(F32)
+                .rearrange("p (b i u) -> p b i u", b=n, u=2),
+                in_=bank[:, 0 : n * 256].rearrange("p (b u i) -> p b i u", b=n, u=2),
+            )
+
+        def quantise_supports(it, q0, n):
+            if q0 == 0:
+                scodes[it] = late.tile([P, 6 * P], U32, name="scodes", align_bytes=64)
+                sscales[it] = late.tile([P, 6 * P], U8, name="sscales", align_bytes=64)
+            cols = slice(q0 * P, (q0 + n) * P)
+            nc.vector.quantize_mx(
+                out=scodes[it][:, cols].bitcast(FP8X4),
+                scales=sscales[it][:, cols],
+                in_=sgrp[it][:, q0 * 512 : (q0 + n) * 512],
+            )
+
+        def project(it, passes, first, last):
+            if first:
+                obank[it] = outp.tile([P, NB], F32, name="o")
+            for j, q in enumerate(passes):
+                cols = slice(q * P, (q + 1) * P)
+                w_cols = slice(q * NB, (q + 1) * NB)
+                nc.tensor.matmul_mx(
+                    out=obank[it][:],
+                    lhsT=scodes[it][:, cols].bitcast(FP8X4),
+                    lhsT_scale=sscales[it][:, cols],
+                    rhs=w_codes[:, w_cols].bitcast(FP8X4),
+                    rhs_scale=w_scales[:, w_cols],
+                    start=(first and j == 0),
+                    stop=(last and j == len(passes) - 1),
+                )
+
+        def store(it):
+            res = work.tile([P, NB], F32, name="res", align_bytes=64)
+            nc.scalar.copy(out=res[:], in_=obank[it][:])
+            nc.sync.dma_start(out=out[0, it * P : (it + 1) * P, :], in_=res[:])
+
+        def weight_values(h, pair):
+            c0 = h * R * F + pair * 1024
+            nc.vector.tensor_tensor(
+                out=w_val[:, c0 : c0 + 1024],
+                in0=w_bytes[:, c0 : c0 + 1024].bitcast(FP8),
+                in1=w_scale[:, pair * 1024 : (pair + 1) * 1024],
+                op=MULT,
+            )
+
+        def turn_weights(q):
+            bank = xtp.tile([P, 512], F32, name="xt")
+            words = w_val[:].bitcast(F32)
+            for h in range(2):
+                for u in range(2):
+                    k0 = (h * 2 + u) * P
+                    w0 = h * (R * F // 2) + q * 256
+                    nc.tensor.transpose(bank[:, k0 : k0 + P], words[:, w0 + u : w0 + 256 : 2], ident[:])
+            nc.scalar.copy(
+                out=w_grp[:, q * 1024 : (q + 1) * 1024].bitcast(F32).rearrange("p (h n u) -> p h n u", h=2, u=2),
+                in_=bank[:].rearrange("p (h u n) -> p h n u", h=2, u=2),
+            )
+
+        def quantise_weights(pair):
+            cols = slice(pair * 512, (pair + 1) * 512)
+            nc.vector.quantize_mx(
+                out=w_codes[:, cols].bitcast(FP8X4),
+                scales=w_scales[:, cols],
+                in_=w_grp[:, pair * 2048 : (pair + 1) * 2048],
+            )
+
+        load(0, 4)
+        nc.sync.dma_start(
+            out=nf_raw[:], in_=node_features[0].rearrange("(c p t) d -> p c t d", p=P, t=4)
+        )
+        load(1, 2)
+        nc.sync.dma_start(
+            out=relf[:], in_=relation_features[0].rearrange("r d -> (r d)").partition_broadcast(P)
+        )
+        for s in range(2, PREFETCH):
+            load(s)
+
+        row_sums(0)
+        for c in range(2):
+            nc.vector.tensor_copy(out=nf_grp[:, c], in_=nf_raw[:, c].rearrange("p t d -> p d t"))
+        nc.vector.quantize_mx(
+            out=nf_codes[:].bitcast(FP8X4),
+            scales=nf_scales[:],
+            in_=nf_grp[:].rearrange("p c d t -> p (c d t)"),
+        )
+
+        project_at = {}
+        for it in range(IT - 1):
+            project_at[max(4 * it + 6, 20 + it)] = it
+        weight_loads = {
+            2: (load_weight_bytes, (0, 0, DE)),
+            3: (load_weight_bytes, (0, DE, DR)),
+            4: (load_weight_bytes, (1, 0, DE)),
+            5: (load_weight_bytes, (1, DE, DR)),
+            6: (load_weight_scale, (0, DE)),
+            8: (load_weight_scale, (DE, DR)),
+        }
+
+        for s in range(STEPS):
+            if s + PREFETCH < STEPS:
+                load(s + PREFETCH)
+            if s in weight_loads:
+                fn, args = weight_loads[s]
+                fn(*args)
+            if s >= 1:
+                quantise(s - 1)
+            turn(s)
+            for q0, at in ((0, 3), (4, 4), (2, 5)):
+                if s >= at and (s - at) % 4 == 0:
+                    turn_supports((s - at) // 4, q0, 2)
+            if 16 <= s < 19:
+                turn_weights(2 * (s - 16))
+                turn_weights(2 * (s - 16) + 1)
+            if s >= 1:
+                tensor_sums(s - 1)
+                aggregate(s - 1)
+                keep_supports(s - 1)
+            if s + 1 < STEPS:
+                row_sums(s + 1)
+            if 10 <= s < 16:
+                weight_values((s - 10) % 2, (s - 10) // 2)
+            if 17 <= s < 20:
+                quantise_weights(s - 17)
+            for q0, at in ((0, 4), (4, 5), (2, 6)):
+                if s >= at and (s - at) % 4 == 0:
+                    quantise_supports((s - at) // 4, q0, 2)
+            if s in project_at:
+                project(project_at[s], range(6), True, True)
+                store(project_at[s])
+
+        it, s = IT - 1, STEPS - 1
+        turn_supports(it, 4, 2)
+        turn_supports(it, 2, 1)
+        for a in range(RG):
+            quantise(s, a, 1)
+            aggregate(s, a, 1)
+        keep_supports(s, 0, 2)
+        keep_supports(s, 2, 2)
+        turn_supports(it, 3, 1)
+        quantise_supports(it, 0, 2)
+        quantise_supports(it, 4, 2)
+        quantise_supports(it, 2, 1)
+        project(it, (0, 1, 4, 5, 2), True, False)
+        quantise_supports(it, 3, 1)
+        project(it, (3,), False, True)
+        store(it)

@@ -15,7 +15,7 @@ RG = 4
 GROUPS = R // RG
 STEPS = IT * GROUPS
 PREFETCH = 5
-TENSOR_SUMS = (2, 1, 1, 0)
+SCALAR_SUMS = tuple(s for s in range(2, STEPS) if s % 8 in (0, 3, 4))
 
 F32 = mybir.dt.float32
 BF16 = mybir.dt.bfloat16
@@ -37,18 +37,16 @@ def tile_relationalgraphconvolution_pa_kernel(
         keep = ctx.enter_context(tc.tile_pool(name="keep", bufs=1))
         rawp = ctx.enter_context(tc.tile_pool(name="rawp", bufs=PREFETCH + 1))
         work = ctx.enter_context(tc.tile_pool(name="work", bufs=2))
+        three = ctx.enter_context(tc.tile_pool(name="three", bufs=3))
         late = ctx.enter_context(tc.tile_pool(name="late", bufs=6))
-        xtp = ctx.enter_context(tc.psum_pool(name="xtp", bufs=4))
+        xtp = ctx.enter_context(tc.psum_pool(name="xtp", bufs=5))
         mxp = ctx.enter_context(tc.psum_pool(name="mxp", bufs=2))
-        rsp = ctx.enter_context(tc.psum_pool(name="rsp", bufs=1))
         outp = ctx.enter_context(tc.psum_pool(name="outp", bufs=1))
         ctx.enter_context(tc.manual_schedule())
 
         ident = keep.tile([P, P], F32, name="ident", align_bytes=64)
         make_identity(nc, ident[:])
 
-        ones = keep.tile([P, 1], BF16, name="ones", align_bytes=64)
-        nc.gpsimd.memset(ones[:], 1.0)
         nf_raw = keep.tile([P, 2, 4, DE], BF16, name="nf_raw", align_bytes=64)
         nf_grp = keep.tile([P, 2, DE, 4], BF16, name="nf_grp", align_bytes=64)
         nf_codes = keep.tile([P, 2 * DE], U32, name="nf_codes", align_bytes=64)
@@ -105,21 +103,34 @@ def tile_relationalgraphconvolution_pa_kernel(
             it, g = s // GROUPS, s % GROUPS
             if g == 0:
                 rs[it] = late.tile([P, R], F32, name="rs")
-                supn[it] = work.tile([P, R * DE], BF16, name="supn", align_bytes=64)
-                supr[it] = work.tile([P, R * DR], BF16, name="supr", align_bytes=64)
-            perm[s] = work.tile([P, RG * N], BF16, name="perm", align_bytes=64)
-            for a in range(RG - TENSOR_SUMS[g]):
-                r = g * RG + a
+                supn[it] = three.tile([P, R * DE], BF16, name="supn", align_bytes=64)
+                supr[it] = three.tile([P, R * DR], BF16, name="supr", align_bytes=64)
+            perm[s] = three.tile([P, RG * N], BF16, name="perm", align_bytes=64)
+
+        def row_sum(s, a):
+            it, g = s // GROUPS, s % GROUPS
+            r = g * RG + a
+            dst = perm[s][:, a * N : (a + 1) * N].rearrange("p (u q e) -> p u q e", u=2, e=2)
+            src = raw[s][:, a, :].rearrange("p (q u e) -> p u q e", u=2, e=2)
+            if a == RG - 1 and s in SCALAR_SUMS:
+                nc.scalar.activation(
+                    out=dst,
+                    in_=src,
+                    func=mybir.ActivationFunctionType.Copy,
+                    accum_out=rs[it][:, r : r + 1],
+                )
+            else:
                 nc.vector.tensor_scalar(
-                    out=perm[s][:, a * N : (a + 1) * N].rearrange("p (u q e) -> p u q e", u=2, e=2),
-                    in0=raw[s][:, a, :].rearrange("p (q u e) -> p u q e", u=2, e=2),
+                    out=dst,
+                    in0=src,
                     scalar1=1.0,
                     scalar2=None,
                     op0=MULT,
                     op1=ADD,
                     accum_out=rs[it][:, r : r + 1],
                 )
-            relation_part(it, g * RG, RG - TENSOR_SUMS[g])
+            if a % 2 == 1:
+                relation_part(it, r - 1, 2)
 
         def relation_part(it, r0, n):
             c0 = r0 * DR
@@ -130,41 +141,15 @@ def tile_relationalgraphconvolution_pa_kernel(
                 op=MULT,
             )
 
-        def tensor_sums(s):
-            it, g = s // GROUPS, s % GROUPS
-            n = TENSOR_SUMS[g]
-            if n == 0:
-                return
-            bank = rsp.tile([P, 512], F32, name="rsb")
-            for b in range(n):
-                a = RG - n + b
-                tile4 = grp[s][:, a * N : (a + 1) * N].rearrange("p (c i t) -> p c i t", c=2, t=4)
-                for c in range(2):
-                    for t in range(4):
-                        nc.tensor.matmul(
-                            bank[:, b : b + 1],
-                            lhsT=tile4[:, c, :, t],
-                            rhs=ones[:],
-                            start=(c == 0 and t == 0),
-                            stop=(c == 1 and t == 3),
-                        )
-            r0 = (g + 1) * RG - n
-            nc.scalar.copy(out=rs[it][:, r0 : r0 + n], in_=bank[:, 0:n])
-            relation_part(it, r0, n)
-
         def turn(s):
-            grp[s] = work.tile([P, RG * N], BF16, name="grp", align_bytes=64)
+            grp[s] = three.tile([P, RG * N], BF16, name="grp", align_bytes=64)
             for a in range(RG):
                 bank = xtp.tile([P, 512], F32, name="xt")
                 for c in range(2):
                     for u in range(2):
                         k0 = (c * 2 + u) * P
-                        if a < RG - TENSOR_SUMS[s % GROUPS]:
-                            w0 = a * 512 + u * 256 + c * P
-                            src = perm[s][:].bitcast(F32)[:, w0 : w0 + P]
-                        else:
-                            src = raw[s][:, a, :].bitcast(F32)[:, c * 256 + u : (c + 1) * 256 : 2]
-                        nc.tensor.transpose(bank[:, k0 : k0 + P], src, ident[:])
+                        w0 = a * 512 + u * 256 + c * P
+                        nc.tensor.transpose(bank[:, k0 : k0 + P], perm[s][:].bitcast(F32)[:, w0 : w0 + P], ident[:])
                 nc.scalar.copy(
                     out=grp[s][:, a * N : (a + 1) * N].bitcast(F32).rearrange("p (c i u) -> p c i u", c=2, u=2),
                     in_=bank[:].rearrange("p (c u i) -> p c i u", c=2, u=2),
@@ -172,8 +157,8 @@ def tile_relationalgraphconvolution_pa_kernel(
 
         def quantise(s, a0=0, n=RG):
             if a0 == 0:
-                codes[s] = work.tile([P, N], U32, name="codes", align_bytes=64)
-                scales[s] = work.tile([P, N], U8, name="scales", align_bytes=64)
+                codes[s] = three.tile([P, N], U32, name="codes", align_bytes=64)
+                scales[s] = three.tile([P, N], U8, name="scales", align_bytes=64)
             cols = slice(a0 * 256, (a0 + n) * 256)
             nc.vector.quantize_mx(
                 out=codes[s][:, cols].bitcast(FP8X4),
@@ -206,7 +191,7 @@ def tile_relationalgraphconvolution_pa_kernel(
                 in_=mx[s][:, a0 * DE : (a0 + n) * DE].rearrange("p (q u e) -> p u q e", u=2, e=2),
             )
 
-        def turn_supports(it, q0, n):
+        def turn_supports(it, q0, n, copy=nc.scalar.copy):
             if q0 == 0:
                 sgrp[it] = work.tile([P, 6 * 512], BF16, name="sgrp", align_bytes=64)
             bank = xtp.tile([P, 512], F32, name="xt")
@@ -221,7 +206,7 @@ def tile_relationalgraphconvolution_pa_kernel(
                         w0 = (q - 4) * 256
                         src = supr[it][:].bitcast(F32)[:, w0 + u : w0 + 256 : 2]
                     nc.tensor.transpose(bank[:, k0 : k0 + P], src, ident[:])
-            nc.scalar.copy(
+            copy(
                 out=sgrp[it][:, q0 * 512 : (q0 + n) * 512]
                 .bitcast(F32)
                 .rearrange("p (b i u) -> p b i u", b=n, u=2),
@@ -302,6 +287,8 @@ def tile_relationalgraphconvolution_pa_kernel(
             load(s)
 
         row_sums(0)
+        for a in range(RG):
+            row_sum(0, a)
         for c in range(2):
             nc.vector.tensor_copy(out=nf_grp[:, c], in_=nf_raw[:, c].rearrange("p t d -> p d t"))
         nc.vector.quantize_mx(
@@ -328,6 +315,9 @@ def tile_relationalgraphconvolution_pa_kernel(
             if s in weight_loads:
                 fn, args = weight_loads[s]
                 fn(*args)
+            if s + 1 < STEPS:
+                row_sums(s + 1)
+                row_sum(s + 1, 0)
             if s >= 1:
                 quantise(s - 1)
             turn(s)
@@ -338,11 +328,8 @@ def tile_relationalgraphconvolution_pa_kernel(
                 turn_weights(2 * (s - 16))
                 turn_weights(2 * (s - 16) + 1)
             if s >= 1:
-                tensor_sums(s - 1)
                 aggregate(s - 1)
                 keep_supports(s - 1)
-            if s + 1 < STEPS:
-                row_sums(s + 1)
             if 10 <= s < 16:
                 weight_values((s - 10) % 2, (s - 10) // 2)
             if 17 <= s < 20:
@@ -350,23 +337,25 @@ def tile_relationalgraphconvolution_pa_kernel(
             for q0, at in ((0, 4), (4, 5), (2, 6)):
                 if s >= at and (s - at) % 4 == 0:
                     quantise_supports((s - at) // 4, q0, 2)
+            if s + 1 < STEPS:
+                for a in range(1, RG):
+                    row_sum(s + 1, a)
             if s in project_at:
                 project(project_at[s], range(6), True, True)
                 store(project_at[s])
 
         it, s = IT - 1, STEPS - 1
-        turn_supports(it, 4, 2)
-        turn_supports(it, 2, 1)
+        turn_supports(it, 4, 2, nc.vector.tensor_copy)
+        turn_supports(it, 2, 1, nc.vector.tensor_copy)
         for a in range(RG):
             quantise(s, a, 1)
             aggregate(s, a, 1)
-        keep_supports(s, 0, 2)
-        keep_supports(s, 2, 2)
-        turn_supports(it, 3, 1)
+        keep_supports(s)
         quantise_supports(it, 0, 2)
         quantise_supports(it, 4, 2)
         quantise_supports(it, 2, 1)
         project(it, (0, 1, 4, 5, 2), True, False)
+        turn_supports(it, 3, 1)
         quantise_supports(it, 3, 1)
         project(it, (3,), False, True)
         store(it)

@@ -15,7 +15,7 @@ RG = 4
 GROUPS = R // RG
 STEPS = IT * GROUPS
 PREFETCH = 5
-SCALAR_SUMS = tuple(s for s in range(2, STEPS) if s % 8 in (0, 3, 4))
+SCALAR_SUMS = (3, 5, 7, 9, 10, 11, 12, 13, 14, 15, 16, 19, 23, 25, 27)
 
 F32 = mybir.dt.float32
 BF16 = mybir.dt.bfloat16
@@ -46,7 +46,14 @@ def tile_relationalgraphconvolution_pa_kernel(
 
         ident = keep.tile([P, P], F32, name="ident", align_bytes=64)
         make_identity(nc, ident[:])
-
+        select = keep.tile([P, 4, P], BF16, name="select", align_bytes=64)
+        nc.vector.memset(select[:], 0.0)
+        for u in range(2):
+            for h in range(2):
+                nc.vector.tensor_copy(
+                    out=select[:, 2 * u + h, :].rearrange("p (b x h) -> p b x h", x=4, h=2)[:, :, :, h],
+                    in_=ident[:].rearrange("p (b u x) -> p b u x", u=2, x=4)[:, :, u, :],
+                )
         nf_raw = keep.tile([P, 2, 4, DE], BF16, name="nf_raw", align_bytes=64)
         nf_grp = keep.tile([P, 2, DE, 4], BF16, name="nf_grp", align_bytes=64)
         nf_codes = keep.tile([P, 2 * DE], U32, name="nf_codes", align_bytes=64)
@@ -99,7 +106,7 @@ def tile_relationalgraphconvolution_pa_kernel(
                 in_=sc[:, f0 : f0 + width].partition_broadcast(P),
             )
 
-        def row_sums(s):
+        def open_step(s):
             it, g = s // GROUPS, s % GROUPS
             if g == 0:
                 rs[it] = late.tile([P, R], F32, name="rs")
@@ -107,11 +114,11 @@ def tile_relationalgraphconvolution_pa_kernel(
                 supr[it] = three.tile([P, R * DR], BF16, name="supr", align_bytes=64)
             perm[s] = three.tile([P, RG * N], BF16, name="perm", align_bytes=64)
 
-        def row_sum(s, a):
+        def reorder(s, a):
             it, g = s // GROUPS, s % GROUPS
             r = g * RG + a
-            dst = perm[s][:, a * N : (a + 1) * N].rearrange("p (u q e) -> p u q e", u=2, e=2)
-            src = raw[s][:, a, :].rearrange("p (q u e) -> p u q e", u=2, e=2)
+            dst = perm[s][:, a * N : (a + 1) * N].rearrange("p (u q f) -> p u q f", u=2, f=16)
+            src = raw[s][:, a, :].rearrange("p (q u f) -> p u q f", u=2, f=16)
             if a == RG - 1 and s in SCALAR_SUMS:
                 nc.scalar.activation(
                     out=dst,
@@ -129,14 +136,14 @@ def tile_relationalgraphconvolution_pa_kernel(
                     op1=ADD,
                     accum_out=rs[it][:, r : r + 1],
                 )
-            if a % 2 == 1:
-                relation_part(it, r - 1, 2)
 
-        def relation_part(it, r0, n):
-            c0 = r0 * DR
+        def relation_part(s, a, n):
+            it, g = s // GROUPS, s % GROUPS
+            r0 = g * RG + a
+            cols = slice(r0 * DR, (r0 + n) * DR)
             nc.gpsimd.tensor_tensor(
-                out=supr[it][:, c0 : c0 + n * DR].rearrange("p (r d) -> p r d", d=DR),
-                in0=relf[:, c0 : c0 + n * DR].rearrange("p (r d) -> p r d", d=DR),
+                out=supr[it][:, cols].rearrange("p (r d) -> p r d", d=DR),
+                in0=relf[:, cols].rearrange("p (r d) -> p r d", d=DR),
                 in1=rs[it][:, r0 : r0 + n].unsqueeze(2).to_broadcast([P, n, DR]),
                 op=MULT,
             )
@@ -286,11 +293,22 @@ def tile_relationalgraphconvolution_pa_kernel(
         for s in range(2, PREFETCH):
             load(s)
 
-        row_sums(0)
+        open_step(0)
         for a in range(RG):
-            row_sum(0, a)
+            reorder(0, a)
+        relation_part(0, 0, RG)
         for c in range(2):
-            nc.vector.tensor_copy(out=nf_grp[:, c], in_=nf_raw[:, c].rearrange("p t d -> p d t"))
+            bank = xtp.tile([P, 512], F32, name="xt")
+            for u in range(2):
+                for h in range(2):
+                    nc.tensor.matmul(
+                        bank[:, u * 256 : (u + 1) * 256],
+                        lhsT=select[:, 2 * u + h, :],
+                        rhs=nf_raw[:, c, 2 * h : 2 * h + 2, :].rearrange("p e d -> p (e d)"),
+                        start=(h == 0),
+                        stop=(h == 1),
+                    )
+            nc.scalar.copy(out=nf_grp[:, c], in_=bank[:].rearrange("p (t d) -> p d t", t=4))
         nc.vector.quantize_mx(
             out=nf_codes[:].bitcast(FP8X4),
             scales=nf_scales[:],
@@ -299,7 +317,7 @@ def tile_relationalgraphconvolution_pa_kernel(
 
         project_at = {}
         for it in range(IT - 1):
-            project_at[max(4 * it + 6, 20 + it)] = it
+            project_at[max(4 * it + 8, 21 + it)] = it
         weight_loads = {
             2: (load_weight_bytes, (0, 0, DE)),
             3: (load_weight_bytes, (0, DE, DR)),
@@ -316,41 +334,49 @@ def tile_relationalgraphconvolution_pa_kernel(
                 fn, args = weight_loads[s]
                 fn(*args)
             if s + 1 < STEPS:
-                row_sums(s + 1)
-                row_sum(s + 1, 0)
+                open_step(s + 1)
+                reorder(s + 1, 0)
             if s >= 1:
                 quantise(s - 1)
             turn(s)
-            for q0, at in ((0, 3), (4, 4), (2, 5)):
+            for q0, at in ((0, 4), (4, 5), (2, 6)):
                 if s >= at and (s - at) % 4 == 0:
                     turn_supports((s - at) // 4, q0, 2)
             if 16 <= s < 19:
                 turn_weights(2 * (s - 16))
                 turn_weights(2 * (s - 16) + 1)
-            if s >= 1:
-                aggregate(s - 1)
-                keep_supports(s - 1)
+            if s >= 2:
+                aggregate(s - 2)
+                keep_supports(s - 2)
             if 10 <= s < 16:
                 weight_values((s - 10) % 2, (s - 10) // 2)
             if 17 <= s < 20:
                 quantise_weights(s - 17)
-            for q0, at in ((0, 4), (4, 5), (2, 6)):
+            for q0, at in ((0, 5), (4, 6), (2, 7)):
                 if s >= at and (s - at) % 4 == 0:
                     quantise_supports((s - at) // 4, q0, 2)
             if s + 1 < STEPS:
-                for a in range(1, RG):
-                    row_sum(s + 1, a)
+                reorder(s + 1, 1)
+                relation_part(s + 1, 0, 2)
+                reorder(s + 1, 2)
+                reorder(s + 1, 3)
+                relation_part(s + 1, 2, 2)
             if s in project_at:
                 project(project_at[s], range(6), True, True)
                 store(project_at[s])
 
         it, s = IT - 1, STEPS - 1
-        turn_supports(it, 4, 2, nc.vector.tensor_copy)
-        turn_supports(it, 2, 1, nc.vector.tensor_copy)
+        project(it - 1, range(6), True, True)
+        store(it - 1)
+        aggregate(s - 1)
+        keep_supports(s - 1)
         for a in range(RG):
             quantise(s, a, 1)
-            aggregate(s, a, 1)
+        turn_supports(it, 0, 2, nc.vector.tensor_copy)
+        turn_supports(it, 4, 2, nc.vector.tensor_copy)
+        aggregate(s)
         keep_supports(s)
+        turn_supports(it, 2, 1, nc.vector.tensor_copy)
         quantise_supports(it, 0, 2)
         quantise_supports(it, 4, 2)
         quantise_supports(it, 2, 1)

from contextlib import ExitStack

import concourse.mybir as mybir
from concourse.masks import make_identity

N = 1024
R = 16
DE = 128
DR = 64
F = DE + DR
NB = 256
P = 128
IT = N // P
RG = 4
GROUPS = R // RG
STEPS = IT * GROUPS
PREFETCH = 5
SCALAR_SUMS = (3, 5, 7, 9, 10, 11, 12, 13, 14, 15, 16, 19, 23, 25, 27)

F32 = mybir.dt.float32
BF16 = mybir.dt.bfloat16
U32 = mybir.dt.uint32
U8 = mybir.dt.uint8
FP8 = mybir.dt.float8_e4m3fn
FP8X4 = mybir.dt.float8_e4m3fn_x4
MULT = mybir.AluOpType.mult
ADD = mybir.AluOpType.add

FLOPS = 2 * (R * N * N * DE + N * R * F * NB)


def tile_relationalgraphconvolution_pa_kernel(
    tc, node_features, relation_features, adj, Wb_bytes, Wb_scale, out
):
    nc = tc.nc
    with ExitStack() as ctx:
        keep = ctx.enter_context(tc.tile_pool(name="keep", bufs=1))
        rawp = ctx.enter_context(tc.tile_pool(name="rawp", bufs=PREFETCH + 1))
        work = ctx.enter_context(tc.tile_pool(name="work", bufs=2))
        three = ctx.enter_context(tc.tile_pool(name="three", bufs=3))
        late = ctx.enter_context(tc.tile_pool(name="late", bufs=6))
        xtp = ctx.enter_context(tc.psum_pool(name="xtp", bufs=5))
        mxp = ctx.enter_context(tc.psum_pool(name="mxp", bufs=2))
        outp = ctx.enter_context(tc.psum_pool(name="outp", bufs=1))
        ctx.enter_context(tc.manual_schedule())

        ident = keep.tile([P, P], F32, name="ident", align_bytes=64)
        make_identity(nc, ident[:])
        select = keep.tile([P, 4, P], BF16, name="select", align_bytes=64)
        nc.vector.memset(select[:], 0.0)
        for u in range(2):
            for h in range(2):
                nc.vector.tensor_copy(
                    out=select[:, 2 * u + h, :].rearrange("p (b x h) -> p b x h", x=4, h=2)[:, :, :, h],
                    in_=ident[:].rearrange("p (b u x) -> p b u x", u=2, x=4)[:, :, u, :],
                )
        nf_raw = keep.tile([P, 2, 4, DE], BF16, name="nf_raw", align_bytes=64)
        nf_grp = keep.tile([P, 2, DE, 4], BF16, name="nf_grp", align_bytes=64)
        nf_codes = keep.tile([P, 2 * DE], U32, name="nf_codes", align_bytes=64)
        nf_scales = keep.tile([P, 2 * DE], U8, name="nf_scales", align_bytes=64)
        relf = keep.tile([P, R * DR], BF16, name="relf", align_bytes=64)
        w_bytes = keep.tile([P, 2 * R * F], U8, name="w_bytes", align_bytes=64)
        w_scale = keep.tile([P, R * F], F32, name="w_scale", align_bytes=64)
        w_val = keep.tile([P, 2 * R * F], BF16, name="w_val", align_bytes=64)
        w_grp = keep.tile([P, 6 * NB * 4], BF16, name="w_grp", align_bytes=64)
        w_codes = keep.tile([P, 6 * NB], U32, name="w_codes", align_bytes=64)
        w_scales = keep.tile([P, 6 * NB], U8, name="w_scales", align_bytes=64)

        raw = {}
        perm = {}
        grp = {}
        codes = {}
        scales = {}
        mx = {}
        rs = {}
        supn = {}
        supr = {}
        sgrp = {}
        scodes = {}
        sscales = {}
        obank = {}

        def load(s, pieces=1):
            it, g = s // GROUPS, s % GROUPS
            raw[s] = rawp.tile([P, RG, N], BF16, name="raw", align_bytes=64)
            n = RG // pieces
            for a in range(pieces):
                r0 = g * RG + a * n
                nc.sync.dma_start(
                    out=raw[s][:, a * n : (a + 1) * n, :],
                    in_=adj[0, r0 : r0 + n, it * P : (it + 1) * P, :].rearrange("r i j -> i r j"),
                )

        def load_weight_bytes(h, f0, width):
            c0 = h * R * F + f0 * R
            rows = Wb_bytes[h * P : (h + 1) * P, :].rearrange("n (r f) -> n r f", f=F)
            nc.sync.dma_start(
                out=w_bytes[:, c0 : c0 + R * width].rearrange("p (r d) -> p r d", d=width),
                in_=rows[:, :, f0 : f0 + width],
            )

        def load_weight_scale(f0, width):
            sc = Wb_scale.rearrange("o (r f) -> (o r) f", f=F)
            nc.sync.dma_start(
                out=w_scale[:, f0 * R : f0 * R + R * width].rearrange("p (r d) -> p r d", d=width),
                in_=sc[:, f0 : f0 + width].partition_broadcast(P),
            )

        def open_step(s):
            it, g = s // GROUPS, s % GROUPS
            if g == 0:
                rs[it] = late.tile([P, R], F32, name="rs")
                supn[it] = three.tile([P, R * DE], BF16, name="supn", align_bytes=64)
                supr[it] = three.tile([P, R * DR], BF16, name="supr", align_bytes=64)
            perm[s] = three.tile([P, RG * N], BF16, name="perm", align_bytes=64)

        def reorder(s, a):
            it, g = s // GROUPS, s % GROUPS
            r = g * RG + a
            dst = perm[s][:, a * N : (a + 1) * N].rearrange("p (u q f) -> p u q f", u=2, f=16)
            src = raw[s][:, a, :].rearrange("p (q u f) -> p u q f", u=2, f=16)
            if a == RG - 1 and s in SCALAR_SUMS:
                nc.scalar.activation(
                    out=dst,
                    in_=src,
                    func=mybir.ActivationFunctionType.Copy,
                    accum_out=rs[it][:, r : r + 1],
                )
            else:
                nc.vector.tensor_scalar(
                    out=dst,
                    in0=src,
                    scalar1=1.0,
                    scalar2=None,
                    op0=MULT,
                    op1=ADD,
                    accum_out=rs[it][:, r : r + 1],
                )

        def relation_part(s, a, n):
            it, g = s // GROUPS, s % GROUPS
            r0 = g * RG + a
            cols = slice(r0 * DR, (r0 + n) * DR)
            nc.gpsimd.tensor_tensor(
                out=supr[it][:, cols].rearrange("p (r d) -> p r d", d=DR),
                in0=relf[:, cols].rearrange("p (r d) -> p r d", d=DR),
                in1=rs[it][:, r0 : r0 + n].unsqueeze(2).to_broadcast([P, n, DR]),
                op=MULT,
            )

        def turn(s):
            grp[s] = three.tile([P, RG * N], BF16, name="grp", align_bytes=64)
            for a in range(RG):
                bank = xtp.tile([P, 512], F32, name="xt")
                for c in range(2):
                    for u in range(2):
                        k0 = (c * 2 + u) * P
                        w0 = a * 512 + u * 256 + c * P
                        nc.tensor.transpose(bank[:, k0 : k0 + P], perm[s][:].bitcast(F32)[:, w0 : w0 + P], ident[:])
                nc.scalar.copy(
                    out=grp[s][:, a * N : (a + 1) * N].bitcast(F32).rearrange("p (c i u) -> p c i u", c=2, u=2),
                    in_=bank[:].rearrange("p (c u i) -> p c i u", c=2, u=2),
                )

        def quantise(s, a0=0, n=RG):
            if a0 == 0:
                codes[s] = three.tile([P, N], U32, name="codes", align_bytes=64)
                scales[s] = three.tile([P, N], U8, name="scales", align_bytes=64)
            cols = slice(a0 * 256, (a0 + n) * 256)
            nc.vector.quantize_mx(
                out=codes[s][:, cols].bitcast(FP8X4),
                scales=scales[s][:, cols],
                in_=grp[s][:, a0 * N : (a0 + n) * N],
            )

        def aggregate(s, a0=0, n=RG):
            if a0 == 0:
                mx[s] = mxp.tile([P, RG * DE], F32, name="mx")
            for a in range(a0, a0 + n):
                for c in range(2):
                    cols = slice(a * 256 + c * P, a * 256 + (c + 1) * P)
                    nf_cols = slice(c * DE, (c + 1) * DE)
                    nc.tensor.matmul_mx(
                        out=mx[s][:, a * DE : (a + 1) * DE],
                        lhsT=codes[s][:, cols].bitcast(FP8X4),
                        lhsT_scale=scales[s][:, cols],
                        rhs=nf_codes[:, nf_cols].bitcast(FP8X4),
                        rhs_scale=nf_scales[:, nf_cols],
                        start=(c == 0),
                        stop=(c == 1),
                    )

        def keep_supports(s, a0=0, n=RG):
            it, g = s // GROUPS, s % GROUPS
            dst = supn[it][:, g * 512 : (g + 1) * 512].rearrange("p (u q e) -> p u q e", u=2, e=2)
            nc.scalar.copy(
                out=dst[:, :, a0 * 32 : (a0 + n) * 32, :],
                in_=mx[s][:, a0 * DE : (a0 + n) * DE].rearrange("p (q u e) -> p u q e", u=2, e=2),
            )

        def turn_supports(it, q0, n, copy=nc.scalar.copy):
            if q0 == 0:
                sgrp[it] = work.tile([P, 6 * 512], BF16, name="sgrp", align_bytes=64)
            bank = xtp.tile([P, 512], F32, name="xt")
            for b in range(n):
                for u in range(2):
                    k0 = (b * 2 + u) * P
                    q = q0 + b
                    if q < 4:
                        w0 = q * 256 + u * P
                        src = supn[it][:].bitcast(F32)[:, w0 : w0 + P]
                    else:
                        w0 = (q - 4) * 256
                        src = supr[it][:].bitcast(F32)[:, w0 + u : w0 + 256 : 2]
                    nc.tensor.transpose(bank[:, k0 : k0 + P], src, ident[:])
            copy(
                out=sgrp[it][:, q0 * 512 : (q0 + n) * 512]
                .bitcast(F32)
                .rearrange("p (b i u) -> p b i u", b=n, u=2),
                in_=bank[:, 0 : n * 256].rearrange("p (b u i) -> p b i u", b=n, u=2),
            )

        def quantise_supports(it, q0, n):
            if q0 == 0:
                scodes[it] = late.tile([P, 6 * P], U32, name="scodes", align_bytes=64)
                sscales[it] = late.tile([P, 6 * P], U8, name="sscales", align_bytes=64)
            cols = slice(q0 * P, (q0 + n) * P)
            nc.vector.quantize_mx(
                out=scodes[it][:, cols].bitcast(FP8X4),
                scales=sscales[it][:, cols],
                in_=sgrp[it][:, q0 * 512 : (q0 + n) * 512],
            )

        def project(it, passes, first, last):
            if first:
                obank[it] = outp.tile([P, NB], F32, name="o")
            for j, q in enumerate(passes):
                cols = slice(q * P, (q + 1) * P)
                w_cols = slice(q * NB, (q + 1) * NB)
                nc.tensor.matmul_mx(
                    out=obank[it][:],
                    lhsT=scodes[it][:, cols].bitcast(FP8X4),
                    lhsT_scale=sscales[it][:, cols],
                    rhs=w_codes[:, w_cols].bitcast(FP8X4),
                    rhs_scale=w_scales[:, w_cols],
                    start=(first and j == 0),
                    stop=(last and j == len(passes) - 1),
                )

        def store(it):
            res = work.tile([P, NB], F32, name="res", align_bytes=64)
            nc.scalar.copy(out=res[:], in_=obank[it][:])
            nc.sync.dma_start(out=out[0, it * P : (it + 1) * P, :], in_=res[:])

        def weight_values(h, pair):
            c0 = h * R * F + pair * 1024
            nc.vector.tensor_tensor(
                out=w_val[:, c0 : c0 + 1024],
                in0=w_bytes[:, c0 : c0 + 1024].bitcast(FP8),
                in1=w_scale[:, pair * 1024 : (pair + 1) * 1024],
                op=MULT,
            )

        def turn_weights(q):
            bank = xtp.tile([P, 512], F32, name="xt")
            words = w_val[:].bitcast(F32)
            for h in range(2):
                for u in range(2):
                    k0 = (h * 2 + u) * P
                    w0 = h * (R * F // 2) + q * 256
                    nc.tensor.transpose(bank[:, k0 : k0 + P], words[:, w0 + u : w0 + 256 : 2], ident[:])
            nc.scalar.copy(
                out=w_grp[:, q * 1024 : (q + 1) * 1024].bitcast(F32).rearrange("p (h n u) -> p h n u", h=2, u=2),
                in_=bank[:].rearrange("p (h u n) -> p h n u", h=2, u=2),
            )

        def quantise_weights(pair):
            cols = slice(pair * 512, (pair + 1) * 512)
            nc.vector.quantize_mx(
                out=w_codes[:, cols].bitcast(FP8X4),
                scales=w_scales[:, cols],
                in_=w_grp[:, pair * 2048 : (pair + 1) * 2048],
            )

        load(0, 4)
        nc.sync.dma_start(
            out=nf_raw[:], in_=node_features[0].rearrange("(c p t) d -> p c t d", p=P, t=4)
        )
        load(1, 2)
        nc.sync.dma_start(
            out=relf[:], in_=relation_features[0].rearrange("r d -> (r d)").partition_broadcast(P)
        )
        for s in range(2, PREFETCH):
            load(s)

        open_step(0)
        for a in range(RG):
            reorder(0, a)
        relation_part(0, 0, RG)
        for c in range(2):
            bank = xtp.tile([P, 512], F32, name="xt")
            for u in range(2):
                for h in range(2):
                    nc.tensor.matmul(
                        bank[:, u * 256 : (u + 1) * 256],
                        lhsT=select[:, 2 * u + h, :],
                        rhs=nf_raw[:, c, 2 * h : 2 * h + 2, :].rearrange("p e d -> p (e d)"),
                        start=(h == 0),
                        stop=(h == 1),
                    )
            nc.scalar.copy(out=nf_grp[:, c], in_=bank[:].rearrange("p (t d) -> p d t", t=4))
        nc.vector.quantize_mx(
            out=nf_codes[:].bitcast(FP8X4),
            scales=nf_scales[:],
            in_=nf_grp[:].rearrange("p c d t -> p (c d t)"),
        )

        project_at = {}
        for it in range(IT - 1):
            project_at[max(4 * it + 8, 21 + it)] = it
        weight_loads = {
            2: (load_weight_bytes, (0, 0, DE)),
            3: (load_weight_bytes, (0, DE, DR)),
            4: (load_weight_bytes, (1, 0, DE)),
            5: (load_weight_bytes, (1, DE, DR)),
            6: (load_weight_scale, (0, DE)),
            8: (load_weight_scale, (DE, DR)),
        }

        for s in range(STEPS):
            if s + PREFETCH < STEPS:
                load(s + PREFETCH)
            if s in weight_loads:
                fn, args = weight_loads[s]
                fn(*args)
            if s + 1 < STEPS:
                open_step(s + 1)
                reorder(s + 1, 0)
            if s >= 1:
                quantise(s - 1)
            turn(s)
            for q0, at in ((0, 4), (4, 5), (2, 6)):
                if s >= at and (s - at) % 4 == 0:
                    turn_supports((s - at) // 4, q0, 2)
            if 16 <= s < 19:
                turn_weights(2 * (s - 16))
                turn_weights(2 * (s - 16) + 1)
            if s >= 2:
                aggregate(s - 2)
                keep_supports(s - 2)
            if 10 <= s < 16:
                weight_values((s - 10) % 2, (s - 10) // 2)
            if 17 <= s < 20:
                quantise_weights(s - 17)
            for q0, at in ((0, 5), (4, 6), (2, 7)):
                if s >= at and (s - at) % 4 == 0:
                    quantise_supports((s - at) // 4, q0, 2)
            if s + 1 < STEPS:
                reorder(s + 1, 1)
                relation_part(s + 1, 0, 2)
                reorder(s + 1, 2)
                reorder(s + 1, 3)
                relation_part(s + 1, 2, 2)
            if s in project_at:
                project(project_at[s], range(6), True, True)
                store(project_at[s])

        it, s = IT - 1, STEPS - 1
        project(it - 1, range(6), True, True)
        store(it - 1)
        aggregate(s - 1)
        keep_supports(s - 1)
        for a in range(RG):
            quantise(s, a, 1)
        turn_supports(it, 0, 2, nc.vector.tensor_copy)
        turn_supports(it, 4, 2, nc.vector.tensor_copy)
        aggregate(s)
        keep_supports(s)
        turn_supports(it, 2, 1, nc.vector.tensor_copy)
        quantise_supports(it, 0, 2)
        quantise_supports(it, 4, 2)
        quantise_supports(it, 2, 1)
        project(it, (0, 1, 4, 5, 2), True, False)
        turn_supports(it, 3, 1)
        quantise_supports(it, 3, 1)
        project(it, (3,), False, True)
        store(it)
